import numpy as np
import ml_dtypes


def mxq(x, axis, fmt="e4m3"):
    dtype, down = {"e4m3": (ml_dtypes.float8_e4m3fn, 7), "e5m2": (ml_dtypes.float8_e5m2, 14)}[fmt]
    v = np.moveaxis(np.asarray(x, np.float32).astype(ml_dtypes.bfloat16).astype(np.float64), axis, -1)
    blocks = v.reshape(v.shape[:-1] + (-1, 32))
    amax = np.abs(blocks).max(-1, keepdims=True)
    byte = np.maximum(np.where(amax > 0, np.frexp(amax)[1] - 1 + 127, 0) - down, 1)
    scale = np.exp2(byte - 127.0)
    codes = (blocks / scale).astype(np.float32).astype(dtype).astype(np.float64)
    return np.moveaxis((codes * scale).reshape(v.shape), -1, axis)


WIDE = False


def mx_kscale(k):
    if not WIDE:
        return np.ones(k)
    levels = np.array([10, -10, 5, -5, 0])
    if k % 512:
        return np.exp2(np.random.permutation(np.resize(levels, k // 32))).repeat(32)
    a = np.empty((k // 512, 16))
    for p in range(k // 512):
        a[p, :8] = np.random.permutation(np.resize(levels, 8))
        for g in range(8):
            far = levels[np.abs(levels - a[p, g]) >= 10]
            a[p, g + 8] = far[np.random.randint(len(far))]
    return np.exp2(a.ravel()).repeat(32)


BF16 = ml_dtypes.bfloat16


def bf(x):
    return np.asarray(x, np.float32).astype(BF16)


def f64(x):
    return np.asarray(x).astype(np.float64)


B, S, D, DFF, R = 4, 2048, 1024, 512, 512


def erf(z):
    z2 = z * z
    acc = np.zeros_like(z)
    for c in (np.arange(13) + 0.5) ** 2 * 0.25:
        acc += np.exp(-c) / (c + z2)
    return np.tanh(2.0 * np.pi * z) - z * np.exp(-z2) / np.pi * acc


def gelu_erf(v):
    return 0.5 * v * (1.0 + erf(v / np.sqrt(2.0)))


def setup_inputs():
    s, r = mx_kscale(D), mx_kscale(R)
    return {"x": bf(np.random.standard_normal((B, S, D)) * s),
            "c_fc_U": bf(np.random.standard_normal((D, R)) * 2.0 / np.sqrt(D) / s[:, None]),
            "c_fc_S": bf(np.random.uniform(size=R) * r),
            "c_fc_V": bf(np.random.standard_normal((DFF, R)) / np.sqrt(R) / r[None, :]),
            "c_fc_bias": bf(np.random.standard_normal(DFF) * 0.3)}


def reference(x, c_fc_U, c_fc_S, c_fc_V, c_fc_bias):
    us = f64(c_fc_U) * f64(c_fc_S)[None, :]
    w = mxq(us, 1, "e4m3") @ mxq(f64(c_fc_V), 1, "e4m3").T
    h = (mxq(f64(x), 2, "e4m3") @ mxq(w, 0, "e4m3")) + f64(c_fc_bias)
    return gelu_erf(h)

@@ -1,0 +1,277 @@
+from contextlib import ExitStack
+
+import concourse.mybir as mybir
+from concourse.masks import make_identity
+
+F32 = mybir.dt.float32
+BF16 = mybir.dt.bfloat16
+U32 = mybir.dt.uint32
+U8 = mybir.dt.uint8
+FP8X4 = mybir.dt.float8_e4m3fn_x4
+GELU = mybir.ActivationFunctionType.Gelu
+MULT = mybir.AluOpType.mult
+ADD = mybir.AluOpType.add
+
+P = 128
+TOKENS = 8192
+D = 1024
+DFF = 512
+RANK = 512
+FLOPS = 2 * D * RANK * DFF + 2 * TOKENS * D * DFF
+
+J = 4
+NG = TOKENS // (P * J)
+XBUFS = 8
+LAG = 3
+FINE_STORES = 3
+WARM = 0
+
+
+def tile_hybridsuperlayer_pa_t_kernel(tc, x, c_fc_U, c_fc_S, c_fc_V, c_fc_bias, out):
+    nc = tc.nc
+    x_groups = x.flatten_outer_dims().rearrange("(n p j) k -> n p (j k)", p=P, j=J)
+    out_groups = out.flatten_outer_dims().rearrange("(n p j) f -> n p (j f)", p=P, j=J)
+
+    with ExitStack() as ctx:
+        ctx.enter_context(tc.manual_schedule())
+        keep = ctx.enter_context(tc.tile_pool(name="keep", bufs=1))
+        xin = ctx.enter_context(tc.tile_pool(name="xin", bufs=XBUFS))
+        xgr = ctx.enter_context(tc.tile_pool(name="xgr", bufs=3))
+        xq = ctx.enter_context(tc.tile_pool(name="xq", bufs=4))
+        res = ctx.enter_context(tc.tile_pool(name="res", bufs=6))
+        ps_t = ctx.enter_context(tc.psum_pool(name="ps_t", bufs=4))
+        ps_a = ctx.enter_context(tc.psum_pool(name="ps_a", bufs=4))
+
+        def copy_on(engine, dst, src):
+            if engine == "V":
+                nc.vector.tensor_copy(out=dst, in_=src)
+            else:
+                nc.scalar.copy(out=dst, in_=src)
+
+        u_sb = keep.tile([P, 4, 2 * RANK], BF16, name="u_sb")
+        v_sb = keep.tile([P, 4, RANK], BF16, name="v_sb")
+        u_view = c_fc_U.rearrange("(g p h e) r -> p g h (e r)", g=2, p=P, h=2, e=2)
+        nc.sync.dma_start(out=u_sb[:, 0:1, :], in_=u_view[:, 0, 0:1, :])
+        nc.sync.dma_start(out=u_sb[:, 1:2, :], in_=u_view[:, 0, 1:2, :])
+        nc.sync.dma_start(out=v_sb[:], in_=c_fc_V.rearrange("(c p) r -> p c r", p=P))
+        nc.sync.dma_start(out=u_sb[:, 2:4, :], in_=u_view[:, 1, :, :])
+
+        x_tiles = {}
+
+        def load(n):
+            x_sb = xin.tile([P, J * D], BF16, name="x_sb", tag="x_sb")
+            nc.sync.dma_start(out=x_sb[:], in_=x_groups[n])
+            x_tiles[n] = x_sb
+
+        for n in range(XBUFS):
+            load(n)
+
+        s_rows = keep.tile([P, RANK], BF16, name="s_rows")
+        b_rows = keep.tile([P, DFF], BF16, name="b_rows")
+        ones = keep.tile([P, P], BF16, name="ones")
+        warm = keep.tile([P, 8], F32, name="warm")
+        ident = keep.tile([P, P], F32, name="ident")
+        nc.vector.memset(s_rows[:], 0.0)
+        nc.vector.memset(b_rows[:], 0.0)
+        nc.vector.memset(ones[:], 1.0)
+        nc.vector.memset(warm[:], 0.0)
+        make_identity(nc, ident[:])
+        nc.scalar.dma_start(out=s_rows[0:1, :], in_=c_fc_S.rearrange("(o r) -> o r", o=1))
+        nc.scalar.dma_start(out=b_rows[0:1, :], in_=c_fc_bias.rearrange("(o f) -> o f", o=1))
+        nc.scalar.activation(out=warm[:], in_=warm[:], func=GELU)
+
+        u_words = u_sb[:].bitcast(F32)
+        v_words = v_sb[:].bitcast(F32)
+        g_u = keep.tile([P, 8 * 512], BF16, name="g_u", align_bytes=64)
+        g_v = keep.tile([P, 4 * 512], BF16, name="g_v", align_bytes=64)
+        g_u_words = g_u[:].bitcast(F32).rearrange("p (m d u) -> p m d u", m=8, d=P, u=2)
+        g_v_words = g_v[:].bitcast(F32).rearrange("p (c f u) -> p c f u", c=4, f=P, u=2)
+        u_codes = keep.tile([P, 8 * P], U32, name="u_codes", align_bytes=64)
+        u_scales = keep.tile([P, 8 * P], U8, name="u_scales", align_bytes=64)
+        v_codes = keep.tile([P, DFF], U32, name="v_codes", align_bytes=64)
+        v_scales = keep.tile([P, DFF], U8, name="v_scales", align_bytes=64)
+        s_col = keep.tile([P, 4], BF16, name="s_col")
+
+        def u_bank(b, engine):
+            tp = ps_t.tile([P, 4, P], F32, name="tp_u", tag="t")
+            for e in range(2):
+                for u in range(2):
+                    nc.tensor.transpose(
+                        tp[:, 2 * e + u, :], u_words[:, b, e * 256 + u : (e + 1) * 256 : 2], ident[:]
+                    )
+            copy_on(engine, g_u_words[:, 2 * b : 2 * b + 2], tp[:].rearrange("p (m u) d -> p m d u", u=2))
+
+        def s_column():
+            s_ps = ps_t.tile([P, 4, P], F32, name="s_ps", tag="t")
+            s_words = s_rows[:].bitcast(F32)
+            for u in range(2):
+                nc.tensor.transpose(s_ps[:, u, :], s_words[:, u::2], ident[:])
+            nc.vector.tensor_copy(
+                out=s_col[:].rearrange("p (u e) -> p u e", e=2), in_=s_ps[:, 0:2, 0:1].bitcast(BF16)
+            )
+
+        def u_half(g):
+            half = g_u[:, 2048 * g : 2048 * (g + 1)]
+            nc.vector.tensor_tensor(
+                out=half.rearrange("p (c t) -> p c t", t=4),
+                in0=half.rearrange("p (c t) -> p c t", t=4),
+                in1=s_col[:].unsqueeze(1).to_broadcast([P, 512, 4]),
+                op=MULT,
+            )
+            nc.vector.quantize_mx(
+                out=u_codes[:, 512 * g : 512 * (g + 1)].bitcast(FP8X4),
+                scales=u_scales[:, 512 * g : 512 * (g + 1)],
+                in_=half,
+            )
+
+        def v_bank(b):
+            tp = ps_t.tile([P, 4, P], F32, name="tp_v", tag="t")
+            for cc in range(2):
+                for u in range(2):
+                    nc.tensor.transpose(
+                        tp[:, 2 * cc + u, :], v_words[:, 2 * b + cc, u::2], ident[:]
+                    )
+            nc.scalar.copy(
+                out=g_v_words[:, 2 * b : 2 * b + 2],
+                in_=tp[:].rearrange("p (c u) f -> p c f u", u=2),
+            )
+
+        if WARM:
+            idle_ps = ps_a.tile([P, P], F32, name="idle_ps", tag="a")
+            for k in range(WARM):
+                nc.tensor.matmul(out=idle_ps[:], lhsT=ones[:], rhs=ones[:], start=True, stop=True)
+
+        u_bank(0, "S")
+        u_bank(1, "V")
+        s_column()
+        v_bank(0)
+        v_bank(1)
+        u_half(0)
+        nc.vector.quantize_mx(out=v_codes[:].bitcast(FP8X4), scales=v_scales[:], in_=g_v[:])
+        u_bank(2, "S")
+        u_bank(3, "S")
+        u_half(1)
+
+        b_ps = ps_a.tile([P, DFF], F32, name="b_ps", tag="a")
+        nc.tensor.matmul(out=b_ps[:], lhsT=ones[:], rhs=b_rows[:], start=True, stop=True)
+        bias_bc = keep.tile([P, DFF], F32, name="bias_bc")
+        nc.scalar.copy(out=bias_bc[:], in_=b_ps[:])
+
+        grouped = {}
+        codes = {}
+
+        def flip(n, j, engine):
+            if j == 0:
+                g_x = xgr.tile([P, J * D], BF16, name="g_x", tag="g_x", align_bytes=64)
+                grouped[n] = g_x
+            words = x_tiles[n][:].bitcast(F32)
+            g_x_words = (
+                grouped[n][:].bitcast(F32).rearrange("p (j g t u) -> p j g t u", j=J, g=2, t=P, u=2)
+            )
+            tp = ps_t.tile([P, 4, P], F32, name="tp_x", tag="t")
+            for q in range(4):
+                lo = j * 512 + (q // 2) * 256 + q % 2
+                hi = j * 512 + (q // 2 + 1) * 256
+                nc.tensor.transpose(tp[:, q, :], words[:, lo:hi:2], ident[:])
+            copy_on(engine, g_x_words[:, j], tp[:].rearrange("p (g u) t -> p g t u", u=2))
+            if j == J - 1 and n + XBUFS < NG:
+                load(n + XBUFS)
+
+        def quantise(n, first, count):
+            if first == 0:
+                x_codes = xq.tile([P, J * 256], U32, name="x_codes", tag="x_codes", align_bytes=64)
+                x_scales = xq.tile([P, J * 256], U8, name="x_scales", tag="x_scales", align_bytes=64)
+                codes[n] = (x_codes, x_scales)
+            x_codes, x_scales = codes[n]
+            nc.vector.quantize_mx(
+                out=x_codes[:, first * 256 : (first + count) * 256].bitcast(FP8X4),
+                scales=x_scales[:, first * 256 : (first + count) * 256],
+                in_=grouped[n][:, first * D : (first + count) * D],
+            )
+
+        g_w = keep.tile([P, 2, DFF, 4], BF16, name="g_w", align_bytes=64)
+        w_codes = keep.tile([P, 2, DFF], U32, name="w_codes", align_bytes=64)
+        w_scales = keep.tile([P, 2, DFF], U8, name="w_scales", align_bytes=64)
+
+        def w_half(g, engines):
+            for c in range(4):
+                wa = ps_a.tile([P, 4, P], F32, name="wa", tag="a")
+                for t in range(4):
+                    lo = (4 * g + t) * P
+                    nc.tensor.matmul_mx(
+                        out=wa[:, t, :],
+                        lhsT=u_codes[:, lo : lo + P].bitcast(FP8X4),
+                        lhsT_scale=u_scales[:, lo : lo + P],
+                        rhs=v_codes[:, c * P : (c + 1) * P].bitcast(FP8X4),
+                        rhs_scale=v_scales[:, c * P : (c + 1) * P],
+                        start=True,
+                        stop=True,
+                    )
+                copy_on(engines[c], g_w[:, g, c * P : (c + 1) * P, :], wa[:].rearrange("p t f -> p f t"))
+            nc.vector.quantize_mx(
+                out=w_codes[:, g, :].bitcast(FP8X4),
+                scales=w_scales[:, g, :],
+                in_=g_w[:, g].rearrange("p f t -> p (f t)"),
+            )
+
+        w_half(0, "SSSV")
+        flip(0, 0, "S")
+        w_half(1, "SVSV")
+        flip(0, 1, "S")
+        quantise(0, 0, 2)
+        flip(0, 2, "S")
+        flip(0, 3, "S")
+        quantise(0, 2, 2)
+
+        waiting = []
+
+        def product(n, o_sb, j):
+            x_codes, x_scales = codes[n]
+            acc = ps_a.tile([P, DFF], F32, name="acc", tag="a")
+            for g in range(2):
+                lo = (2 * j + g) * P
+                nc.tensor.matmul_mx(
+                    out=acc[:],
+                    lhsT=x_codes[:, lo : lo + P].bitcast(FP8X4),
+                    lhsT_scale=x_scales[:, lo : lo + P],
+                    rhs=w_codes[:, g, :].bitcast(FP8X4),
+                    rhs_scale=w_scales[:, g, :],
+                    start=(g == 0),
+                    stop=(g == 1),
+                )
+            pieces = 2 if (n == NG - 1 and j == J - 1) else 1
+            width = DFF // pieces
+            for h in range(pieces):
+                nc.vector.tensor_tensor(
+                    out=o_sb[:, j * DFF + h * width : j * DFF + (h + 1) * width],
+                    in0=acc[:, h * width : (h + 1) * width],
+                    in1=bias_bc[:, h * width : (h + 1) * width],
+                    op=ADD,
+                )
+            waiting.append((n, o_sb, j, pieces))
+
+        def finish(i):
+            n, o_sb, j, pieces = waiting[i]
+            width = DFF // pieces
+            for h in range(pieces):
+                lo = j * DFF + h * width
+                cols = o_sb[:, lo : lo + width]
+                nc.scalar.activation(out=cols, in_=cols, func=GELU)
+                if n >= NG - FINE_STORES:
+                    nc.sync.dma_start(out=out_groups[n][:, lo : lo + width], in_=cols)
+            if n < NG - FINE_STORES and j == J - 1:
+                nc.sync.dma_start(out=out_groups[n], in_=o_sb[:])
+
+        for n in range(NG):
+            if n + 1 < NG:
+                for j in range(J):
+                    flip(n + 1, j, "V" if (j == J - 1 and (n + 1) % 5 != 1) else "S")
+            o_sb = res.tile([P, J * DFF], F32, name="o_sb", tag="o_sb")
+            for j in range(J):
+                if j == 1 and n + 1 < NG:
+                    quantise(n + 1, 0, J)
+                product(n, o_sb, j)
+                if n * J + j >= LAG:
+                    finish(n * J + j - LAG)
+        for i in range(NG * J - LAG, NG * J):
+            finish(i)

@@ -24,7 +24,8 @@ NG = TOKENS // (P * J)
 XBUFS = 8
 LAG = 3
 FINE_STORES = 3
-WARM = 0
+ARRANGED = (1, 3)
+AHEAD = 3
 
 
 def tile_hybridsuperlayer_pa_t_kernel(tc, x, c_fc_U, c_fc_S, c_fc_V, c_fc_bias, out):
@@ -36,6 +37,7 @@ def tile_hybridsuperlayer_pa_t_kernel(tc, x, c_fc_U, c_fc_S, c_fc_V, c_fc_bias, 
         ctx.enter_context(tc.manual_schedule())
         keep = ctx.enter_context(tc.tile_pool(name="keep", bufs=1))
         xin = ctx.enter_context(tc.tile_pool(name="xin", bufs=XBUFS))
+        xar = ctx.enter_context(tc.tile_pool(name="xar", bufs=AHEAD))
         xgr = ctx.enter_context(tc.tile_pool(name="xgr", bufs=3))
         xq = ctx.enter_context(tc.tile_pool(name="xq", bufs=4))
         res = ctx.enter_context(tc.tile_pool(name="res", bufs=6))
@@ -50,35 +52,37 @@ def tile_hybridsuperlayer_pa_t_kernel(tc, x, c_fc_U, c_fc_S, c_fc_V, c_fc_bias, 
 
         u_sb = keep.tile([P, 4, 2 * RANK], BF16, name="u_sb")
         v_sb = keep.tile([P, 4, RANK], BF16, name="v_sb")
-        u_view = c_fc_U.rearrange("(g p h e) r -> p g h (e r)", g=2, p=P, h=2, e=2)
-        nc.sync.dma_start(out=u_sb[:, 0:1, :], in_=u_view[:, 0, 0:1, :])
-        nc.sync.dma_start(out=u_sb[:, 1:2, :], in_=u_view[:, 0, 1:2, :])
-        nc.sync.dma_start(out=v_sb[:], in_=c_fc_V.rearrange("(c p) r -> p c r", p=P))
-        nc.sync.dma_start(out=u_sb[:, 2:4, :], in_=u_view[:, 1, :, :])
-
-        x_tiles = {}
-
-        def load(n):
-            x_sb = xin.tile([P, J * D], BF16, name="x_sb", tag="x_sb")
-            nc.sync.dma_start(out=x_sb[:], in_=x_groups[n])
-            x_tiles[n] = x_sb
-
-        for n in range(XBUFS):
-            load(n)
-
-        s_rows = keep.tile([P, RANK], BF16, name="s_rows")
+        s_col = keep.tile([P, 4], BF16, name="s_col")
         b_rows = keep.tile([P, DFF], BF16, name="b_rows")
         ones = keep.tile([P, P], BF16, name="ones")
         warm = keep.tile([P, 8], F32, name="warm")
         ident = keep.tile([P, P], F32, name="ident")
-        nc.vector.memset(s_rows[:], 0.0)
+        nc.vector.memset(warm[:], 0.0)
         nc.vector.memset(b_rows[:], 0.0)
         nc.vector.memset(ones[:], 1.0)
-        nc.vector.memset(warm[:], 0.0)
         make_identity(nc, ident[:])
-        nc.scalar.dma_start(out=s_rows[0:1, :], in_=c_fc_S.rearrange("(o r) -> o r", o=1))
-        nc.scalar.dma_start(out=b_rows[0:1, :], in_=c_fc_bias.rearrange("(o f) -> o f", o=1))
+
+        u_view = c_fc_U.rearrange("(g p h e) r -> p g h (e r)", g=2, p=P, h=2, e=2)
+        nc.scalar.dma_start(out=s_col[:], in_=c_fc_S.rearrange("(p t) -> p t", t=4))
         nc.scalar.activation(out=warm[:], in_=warm[:], func=GELU)
+        nc.sync.dma_start(out=u_sb[:, 0:1, :], in_=u_view[:, 0, 0:1, :])
+        nc.sync.dma_start(out=u_sb[:, 1:2, :], in_=u_view[:, 0, 1:2, :])
+        nc.sync.dma_start(out=v_sb[:], in_=c_fc_V.rearrange("(c p) r -> p c r", p=P))
+        nc.sync.dma_start(out=b_rows[0:1, :], in_=c_fc_bias.rearrange("(o f) -> o f", o=1))
+        nc.sync.dma_start(out=u_sb[:, 2:4, :], in_=u_view[:, 1, :, :])
+
+        x_tiles = {}
+
+        def load(n, pieces=1):
+            x_sb = xin.tile([P, J * D], BF16, name="x_sb", tag="x_sb")
+            width = J * D // pieces
+            for h in range(pieces):
+                cols = slice(h * width, (h + 1) * width)
+                nc.sync.dma_start(out=x_sb[:, cols], in_=x_groups[n][:, cols])
+            x_tiles[n] = x_sb
+
+        for n in range(XBUFS):
+            load(n, pieces=4 if n == 0 else 1)
 
         u_words = u_sb[:].bitcast(F32)
         v_words = v_sb[:].bitcast(F32)
@@ -90,90 +94,89 @@ def tile_hybridsuperlayer_pa_t_kernel(tc, x, c_fc_U, c_fc_S, c_fc_V, c_fc_bias, 
         u_scales = keep.tile([P, 8 * P], U8, name="u_scales", align_bytes=64)
         v_codes = keep.tile([P, DFF], U32, name="v_codes", align_bytes=64)
         v_scales = keep.tile([P, DFF], U8, name="v_scales", align_bytes=64)
-        s_col = keep.tile([P, 4], BF16, name="s_col")
+        banks = {}
 
-        def u_bank(b, engine):
+        def u_flip(b):
             tp = ps_t.tile([P, 4, P], F32, name="tp_u", tag="t")
             for e in range(2):
                 for u in range(2):
                     nc.tensor.transpose(
                         tp[:, 2 * e + u, :], u_words[:, b, e * 256 + u : (e + 1) * 256 : 2], ident[:]
                     )
-            copy_on(engine, g_u_words[:, 2 * b : 2 * b + 2], tp[:].rearrange("p (m u) d -> p m d u", u=2))
+            banks["u", b] = tp
 
-        def s_column():
-            s_ps = ps_t.tile([P, 4, P], F32, name="s_ps", tag="t")
-            s_words = s_rows[:].bitcast(F32)
-            for u in range(2):
-                nc.tensor.transpose(s_ps[:, u, :], s_words[:, u::2], ident[:])
-            nc.vector.tensor_copy(
-                out=s_col[:].rearrange("p (u e) -> p u e", e=2), in_=s_ps[:, 0:2, 0:1].bitcast(BF16)
+        def u_copy(b, engine):
+            copy_on(
+                engine,
+                g_u_words[:, 2 * b : 2 * b + 2],
+                banks["u", b][:].rearrange("p (m u) d -> p m d u", u=2),
             )
 
-        def u_half(g):
-            half = g_u[:, 2048 * g : 2048 * (g + 1)]
+        def u_scale(b):
+            part = g_u[:, 1024 * b : 1024 * (b + 1)].rearrange("p (c t) -> p c t", t=4)
             nc.vector.tensor_tensor(
-                out=half.rearrange("p (c t) -> p c t", t=4),
-                in0=half.rearrange("p (c t) -> p c t", t=4),
-                in1=s_col[:].unsqueeze(1).to_broadcast([P, 512, 4]),
-                op=MULT,
+                out=part, in0=part, in1=s_col[:].unsqueeze(1).to_broadcast([P, 256, 4]), op=MULT
             )
+
+        def u_quantise(g):
             nc.vector.quantize_mx(
                 out=u_codes[:, 512 * g : 512 * (g + 1)].bitcast(FP8X4),
                 scales=u_scales[:, 512 * g : 512 * (g + 1)],
-                in_=half,
+                in_=g_u[:, 2048 * g : 2048 * (g + 1)],
             )
 
-        def v_bank(b):
+        def v_flip(b):
             tp = ps_t.tile([P, 4, P], F32, name="tp_v", tag="t")
             for cc in range(2):
                 for u in range(2):
-                    nc.tensor.transpose(
-                        tp[:, 2 * cc + u, :], v_words[:, 2 * b + cc, u::2], ident[:]
-                    )
-            nc.scalar.copy(
-                out=g_v_words[:, 2 * b : 2 * b + 2],
-                in_=tp[:].rearrange("p (c u) f -> p c f u", u=2),
+                    nc.tensor.transpose(tp[:, 2 * cc + u, :], v_words[:, 2 * b + cc, u::2], ident[:])
+            banks["v", b] = tp
+
+        def v_copy(b, engine):
+            copy_on(
+                engine,
+                g_v_words[:, 2 * b : 2 * b + 2],
+                banks["v", b][:].rearrange("p (c u) f -> p c f u", u=2),
             )
 
-        if WARM:
-            idle_ps = ps_a.tile([P, P], F32, name="idle_ps", tag="a")
-            for k in range(WARM):
-                nc.tensor.matmul(out=idle_ps[:], lhsT=ones[:], rhs=ones[:], start=True, stop=True)
-
-        u_bank(0, "S")
-        u_bank(1, "V")
-        s_column()
-        v_bank(0)
-        v_bank(1)
-        u_half(0)
-        nc.vector.quantize_mx(out=v_codes[:].bitcast(FP8X4), scales=v_scales[:], in_=g_v[:])
-        u_bank(2, "S")
-        u_bank(3, "S")
-        u_half(1)
-
-        b_ps = ps_a.tile([P, DFF], F32, name="b_ps", tag="a")
-        nc.tensor.matmul(out=b_ps[:], lhsT=ones[:], rhs=b_rows[:], start=True, stop=True)
-        bias_bc = keep.tile([P, DFF], F32, name="bias_bc")
-        nc.scalar.copy(out=bias_bc[:], in_=b_ps[:])
+        def v_quantise():
+            nc.vector.quantize_mx(out=v_codes[:].bitcast(FP8X4), scales=v_scales[:], in_=g_v[:])
 
         grouped = {}
         codes = {}
 
-        def flip(n, j, engine):
-            if j == 0:
-                g_x = xgr.tile([P, J * D], BF16, name="g_x", tag="g_x", align_bytes=64)
-                grouped[n] = g_x
+        arranged = {}
+
+        def arrange(n):
+            x_ar = xar.tile([P, len(ARRANGED), 512], U32, name="x_ar", tag="x_ar")
+            words = x_tiles[n][:].bitcast(U32).rearrange("p (j g w u) -> p j g u w", j=J, g=2, u=2)
+            for i, j in enumerate(ARRANGED):
+                nc.gpsimd.tensor_copy(
+                    out=x_ar[:, i, :].rearrange("p (g u w) -> p g u w", g=2, u=2), in_=words[:, j]
+                )
+                arranged[n, j] = x_ar[:, i, :]
+
+        def flip(n, j):
             words = x_tiles[n][:].bitcast(F32)
-            g_x_words = (
-                grouped[n][:].bitcast(F32).rearrange("p (j g t u) -> p j g t u", j=J, g=2, t=P, u=2)
-            )
             tp = ps_t.tile([P, 4, P], F32, name="tp_x", tag="t")
             for q in range(4):
+                if (n, j) in arranged:
+                    cols = arranged[n, j][:, q * P : (q + 1) * P].bitcast(F32)
+                    nc.tensor.transpose(tp[:, q, :], cols, ident[:])
+                    continue
                 lo = j * 512 + (q // 2) * 256 + q % 2
                 hi = j * 512 + (q // 2 + 1) * 256
                 nc.tensor.transpose(tp[:, q, :], words[:, lo:hi:2], ident[:])
-            copy_on(engine, g_x_words[:, j], tp[:].rearrange("p (g u) t -> p g t u", u=2))
+            banks["x", n, j] = tp
+
+        def regroup(n, j, engine):
+            if j == 0:
+                g_x = xgr.tile([P, J * D], BF16, name="g_x", tag="g_x", align_bytes=64)
+                grouped[n] = g_x
+            g_x_words = (
+                grouped[n][:].bitcast(F32).rearrange("p (j g t u) -> p j g t u", j=J, g=2, t=P, u=2)
+            )
+            copy_on(engine, g_x_words[:, j], banks["x", n, j][:].rearrange("p (g u) t -> p g t u", u=2))
             if j == J - 1 and n + XBUFS < NG:
                 load(n + XBUFS)
 
@@ -193,35 +196,83 @@ def tile_hybridsuperlayer_pa_t_kernel(tc, x, c_fc_U, c_fc_S, c_fc_V, c_fc_bias, 
         w_codes = keep.tile([P, 2, DFF], U32, name="w_codes", align_bytes=64)
         w_scales = keep.tile([P, 2, DFF], U8, name="w_scales", align_bytes=64)
 
-        def w_half(g, engines):
-            for c in range(4):
-                wa = ps_a.tile([P, 4, P], F32, name="wa", tag="a")
-                for t in range(4):
-                    lo = (4 * g + t) * P
-                    nc.tensor.matmul_mx(
-                        out=wa[:, t, :],
-                        lhsT=u_codes[:, lo : lo + P].bitcast(FP8X4),
-                        lhsT_scale=u_scales[:, lo : lo + P],
-                        rhs=v_codes[:, c * P : (c + 1) * P].bitcast(FP8X4),
-                        rhs_scale=v_scales[:, c * P : (c + 1) * P],
-                        start=True,
-                        stop=True,
-                    )
-                copy_on(engines[c], g_w[:, g, c * P : (c + 1) * P, :], wa[:].rearrange("p t f -> p f t"))
+        def w_product(g, c):
+            wa = ps_a.tile([P, 4, P], F32, name="wa", tag="a")
+            for t in range(4):
+                lo = (4 * g + t) * P
+                nc.tensor.matmul_mx(
+                    out=wa[:, t, :],
+                    lhsT=u_codes[:, lo : lo + P].bitcast(FP8X4),
+                    lhsT_scale=u_scales[:, lo : lo + P],
+                    rhs=v_codes[:, c * P : (c + 1) * P].bitcast(FP8X4),
+                    rhs_scale=v_scales[:, c * P : (c + 1) * P],
+                    start=True,
+                    stop=True,
+                )
+            banks["w", g, c] = wa
+
+        def w_copy(g, c, engine):
+            copy_on(
+                engine, g_w[:, g, c * P : (c + 1) * P, :], banks["w", g, c][:].rearrange("p t f -> p f t")
+            )
+
+        def w_quantise(g):
             nc.vector.quantize_mx(
                 out=w_codes[:, g, :].bitcast(FP8X4),
                 scales=w_scales[:, g, :],
                 in_=g_w[:, g].rearrange("p f t -> p (f t)"),
             )
 
-        w_half(0, "SSSV")
-        flip(0, 0, "S")
-        w_half(1, "SVSV")
-        flip(0, 1, "S")
+        for n in range(1, AHEAD):
+            arrange(n)
+        u_flip(0)
+        u_copy(0, "S")
+        u_flip(1)
+        u_copy(1, "V")
+        u_scale(0)
+        v_flip(0)
+        v_copy(0, "S")
+        v_flip(1)
+        v_copy(1, "S")
+        u_scale(1)
+        v_quantise()
+        u_flip(2)
+        u_copy(2, "S")
+        u_quantise(0)
+        u_flip(3)
+        u_copy(3, "S")
+        u_scale(2)
+        flip(0, 0)
+        regroup(0, 0, "S")
+        for c in range(4):
+            w_product(0, c)
+        u_scale(3)
+        w_copy(0, 0, "S")
+        w_copy(0, 1, "V")
+        u_quantise(1)
+        w_copy(0, 2, "S")
+        w_copy(0, 3, "V")
+        flip(0, 1)
+        flip(0, 2)
+        flip(0, 3)
+        for c in range(4):
+            w_product(1, c)
+        regroup(0, 1, "S")
+        w_quantise(0)
         quantise(0, 0, 2)
-        flip(0, 2, "S")
-        flip(0, 3, "S")
+        w_copy(1, 0, "S")
+        w_copy(1, 1, "V")
+        w_copy(1, 2, "S")
+        w_copy(1, 3, "V")
+        regroup(0, 2, "S")
+        w_quantise(1)
+        regroup(0, 3, "S")
         quantise(0, 2, 2)
+
+        b_ps = ps_a.tile([P, DFF], F32, name="b_ps", tag="a")
+        nc.tensor.matmul(out=b_ps[:], lhsT=ones[:], rhs=b_rows[:], start=True, stop=True)
+        bias_bc = keep.tile([P, DFF], F32, name="bias_bc")
+        nc.scalar.copy(out=bias_bc[:], in_=b_ps[:])
 
         waiting = []
 
@@ -263,9 +314,12 @@ def tile_hybridsuperlayer_pa_t_kernel(tc, x, c_fc_U, c_fc_S, c_fc_V, c_fc_bias, 
                 nc.sync.dma_start(out=out_groups[n], in_=o_sb[:])
 
         for n in range(NG):
+            if n + AHEAD < NG:
+                arrange(n + AHEAD)
             if n + 1 < NG:
                 for j in range(J):
-                    flip(n + 1, j, "V" if (j == J - 1 and (n + 1) % 5 != 1) else "S")
+                    flip(n + 1, j)
+                    regroup(n + 1, j, "V" if (j == J - 1 and (n + 1) % 5 != 1) else "S")
             o_sb = res.tile([P, J * DFF], F32, name="o_sb", tag="o_sb")
             for j in range(J):
                 if j == 1 and n + 1 < NG:

@@ -25,7 +25,7 @@ XBUFS = 8
 LAG = 3
 FINE_STORES = 3
 ARRANGED = (1, 3)
-AHEAD = 3
+LEAD = 2
 
 
 def tile_hybridsuperlayer_pa_t_kernel(tc, x, c_fc_U, c_fc_S, c_fc_V, c_fc_bias, out):
@@ -37,7 +37,7 @@ def tile_hybridsuperlayer_pa_t_kernel(tc, x, c_fc_U, c_fc_S, c_fc_V, c_fc_bias, 
         ctx.enter_context(tc.manual_schedule())
         keep = ctx.enter_context(tc.tile_pool(name="keep", bufs=1))
         xin = ctx.enter_context(tc.tile_pool(name="xin", bufs=XBUFS))
-        xar = ctx.enter_context(tc.tile_pool(name="xar", bufs=AHEAD))
+        xar = ctx.enter_context(tc.tile_pool(name="xar", bufs=2))
         xgr = ctx.enter_context(tc.tile_pool(name="xgr", bufs=3))
         xq = ctx.enter_context(tc.tile_pool(name="xq", bufs=4))
         res = ctx.enter_context(tc.tile_pool(name="res", bufs=6))
@@ -151,7 +151,7 @@ def tile_hybridsuperlayer_pa_t_kernel(tc, x, c_fc_U, c_fc_S, c_fc_V, c_fc_bias, 
             x_ar = xar.tile([P, len(ARRANGED), 512], U32, name="x_ar", tag="x_ar")
             words = x_tiles[n][:].bitcast(U32).rearrange("p (j g w u) -> p j g u w", j=J, g=2, u=2)
             for i, j in enumerate(ARRANGED):
-                nc.gpsimd.tensor_copy(
+                nc.vector.tensor_copy(
                     out=x_ar[:, i, :].rearrange("p (g u w) -> p g u w", g=2, u=2), in_=words[:, j]
                 )
                 arranged[n, j] = x_ar[:, i, :]
@@ -223,8 +223,6 @@ def tile_hybridsuperlayer_pa_t_kernel(tc, x, c_fc_U, c_fc_S, c_fc_V, c_fc_bias, 
                 in_=g_w[:, g].rearrange("p f t -> p (f t)"),
             )
 
-        for n in range(1, AHEAD):
-            arrange(n)
         u_flip(0)
         u_copy(0, "S")
         u_flip(1)
@@ -268,6 +266,10 @@ def tile_hybridsuperlayer_pa_t_kernel(tc, x, c_fc_U, c_fc_S, c_fc_V, c_fc_bias, 
         w_quantise(1)
         regroup(0, 3, "S")
         quantise(0, 2, 2)
+        for j in range(J):
+            flip(1, j)
+            regroup(1, j, "SV"[j % 2])
+        arrange(2)
 
         b_ps = ps_a.tile([P, DFF], F32, name="b_ps", tag="a")
         nc.tensor.matmul(out=b_ps[:], lhsT=ones[:], rhs=b_rows[:], start=True, stop=True)
@@ -314,16 +316,16 @@ def tile_hybridsuperlayer_pa_t_kernel(tc, x, c_fc_U, c_fc_S, c_fc_V, c_fc_bias, 
                 nc.sync.dma_start(out=out_groups[n], in_=o_sb[:])
 
         for n in range(NG):
-            if n + AHEAD < NG:
-                arrange(n + AHEAD)
             if n + 1 < NG:
+                quantise(n + 1, 0, J)
+            if n + LEAD < NG:
                 for j in range(J):
-                    flip(n + 1, j)
-                    regroup(n + 1, j, "V" if (j == J - 1 and (n + 1) % 5 != 1) else "S")
+                    flip(n + LEAD, j)
+                    regroup(n + LEAD, j, "V" if (j == J - 1 and n % 2 == 0) else "S")
+            if n + LEAD + 1 < NG:
+                arrange(n + LEAD + 1)
             o_sb = res.tile([P, J * DFF], F32, name="o_sb", tag="o_sb")
             for j in range(J):
-                if j == 1 and n + 1 < NG:
-                    quantise(n + 1, 0, J)
                 product(n, o_sb, j)
                 if n * J + j >= LAG:
                     finish(n * J + j - LAG)

@@ -22,8 +22,8 @@ FLOPS = 2 * D * RANK * DFF + 2 * TOKENS * D * DFF
 J = 4
 NG = TOKENS // (P * J)
 XBUFS = 8
-LAG = 3
-FINE_STORES = 3
+LAG = 2
+FINE_STORES = 1
 ARRANGED = (1, 3)
 LEAD = 2
 
@@ -149,10 +149,10 @@ def tile_hybridsuperlayer_pa_t_kernel(tc, x, c_fc_U, c_fc_S, c_fc_V, c_fc_bias, 
 
         def arrange(n):
             x_ar = xar.tile([P, len(ARRANGED), 512], U32, name="x_ar", tag="x_ar")
-            words = x_tiles[n][:].bitcast(U32).rearrange("p (j g w u) -> p j g u w", j=J, g=2, u=2)
+            words = x_tiles[n][:].bitcast(U32).rearrange("p (j g w u) -> p j g w u", j=J, g=2, u=2)
             for i, j in enumerate(ARRANGED):
                 nc.vector.tensor_copy(
-                    out=x_ar[:, i, :].rearrange("p (g u w) -> p g u w", g=2, u=2), in_=words[:, j]
+                    out=x_ar[:, i, :].rearrange("p (g u w) -> p g w u", g=2, u=2), in_=words[:, j]
                 )
                 arranged[n, j] = x_ar[:, i, :]
 
@@ -271,6 +271,7 @@ def tile_hybridsuperlayer_pa_t_kernel(tc, x, c_fc_U, c_fc_S, c_fc_V, c_fc_bias, 
             regroup(1, j, "SV"[j % 2])
         arrange(2)
 
+
         b_ps = ps_a.tile([P, DFF], F32, name="b_ps", tag="a")
         nc.tensor.matmul(out=b_ps[:], lhsT=ones[:], rhs=b_rows[:], start=True, stop=True)
         bias_bc = keep.tile([P, DFF], F32, name="bias_bc")
@@ -312,22 +313,33 @@ def tile_hybridsuperlayer_pa_t_kernel(tc, x, c_fc_U, c_fc_S, c_fc_V, c_fc_bias, 
                 nc.scalar.activation(out=cols, in_=cols, func=GELU)
                 if n >= NG - FINE_STORES:
                     nc.sync.dma_start(out=out_groups[n][:, lo : lo + width], in_=cols)
-            if n < NG - FINE_STORES and j == J - 1:
-                nc.sync.dma_start(out=out_groups[n], in_=o_sb[:])
+            if n < NG - FINE_STORES and j % 2 == 1:
+                both = slice((j - 1) * DFF, (j + 1) * DFF)
+                nc.sync.dma_start(out=out_groups[n][:, both], in_=o_sb[:, both])
 
-        for n in range(NG):
-            if n + 1 < NG:
-                quantise(n + 1, 0, J)
-            if n + LEAD < NG:
-                for j in range(J):
-                    flip(n + LEAD, j)
-                    regroup(n + LEAD, j, "V" if (j == J - 1 and n % 2 == 0) else "S")
-            if n + LEAD + 1 < NG:
-                arrange(n + LEAD + 1)
+        def multiply_group(n):
             o_sb = res.tile([P, J * DFF], F32, name="o_sb", tag="o_sb")
             for j in range(J):
                 product(n, o_sb, j)
                 if n * J + j >= LAG:
                     finish(n * J + j - LAG)
+
+        def transpose_group(n, engines):
+            for j in range(J):
+                flip(n, j)
+                regroup(n, j, engines[j])
+
+        multiply_group(0)
+        quantise(1, 0, J)
+        transpose_group(2, "SSSS")
+        arrange(3)
+        for n in range(1, NG):
+            if n + 1 < NG:
+                quantise(n + 1, 0, J)
+            if n + LEAD < NG:
+                transpose_group(n + LEAD, "SSSV" if n % 3 == 1 else "SSSS")
+            if n + LEAD + 1 < NG:
+                arrange(n + LEAD + 1)
+            multiply_group(n)
         for i in range(NG * J - LAG, NG * J):
             finish(i)

@@ -67,7 +67,9 @@ def tile_hybridsuperlayer_pa_t_kernel(tc, x, c_fc_U, c_fc_S, c_fc_V, c_fc_bias, 
         nc.scalar.activation(out=warm[:], in_=warm[:], func=GELU)
         nc.sync.dma_start(out=u_sb[:, 0:1, :], in_=u_view[:, 0, 0:1, :])
         nc.sync.dma_start(out=u_sb[:, 1:2, :], in_=u_view[:, 0, 1:2, :])
-        nc.sync.dma_start(out=v_sb[:], in_=c_fc_V.rearrange("(c p) r -> p c r", p=P))
+        v_view = c_fc_V.rearrange("(c p) r -> p c r", p=P)
+        nc.sync.dma_start(out=v_sb[:, 0:2, :], in_=v_view[:, 0:2, :])
+        nc.sync.dma_start(out=v_sb[:, 2:4, :], in_=v_view[:, 2:4, :])
         nc.sync.dma_start(out=b_rows[0:1, :], in_=c_fc_bias.rearrange("(o f) -> o f", o=1))
         nc.sync.dma_start(out=u_sb[:, 2:4, :], in_=u_view[:, 1, :, :])
 
@@ -88,7 +90,6 @@ def tile_hybridsuperlayer_pa_t_kernel(tc, x, c_fc_U, c_fc_S, c_fc_V, c_fc_bias, 
         v_words = v_sb[:].bitcast(F32)
         g_u = keep.tile([P, 8 * 512], BF16, name="g_u", align_bytes=64)
         g_v = keep.tile([P, 4 * 512], BF16, name="g_v", align_bytes=64)
-        g_u_words = g_u[:].bitcast(F32).rearrange("p (m d u) -> p m d u", m=8, d=P, u=2)
         g_v_words = g_v[:].bitcast(F32).rearrange("p (c f u) -> p c f u", c=4, f=P, u=2)
         u_codes = keep.tile([P, 8 * P], U32, name="u_codes", align_bytes=64)
         u_scales = keep.tile([P, 8 * P], U8, name="u_scales", align_bytes=64)
@@ -105,18 +106,19 @@ def tile_hybridsuperlayer_pa_t_kernel(tc, x, c_fc_U, c_fc_S, c_fc_V, c_fc_bias, 
                     )
             banks["u", b] = tp
 
-        def u_copy(b, engine):
-            copy_on(
-                engine,
-                g_u_words[:, 2 * b : 2 * b + 2],
-                banks["u", b][:].rearrange("p (m u) d -> p m d u", u=2),
-            )
-
         def u_scale(b):
-            part = g_u[:, 1024 * b : 1024 * (b + 1)].rearrange("p (c t) -> p c t", t=4)
-            nc.vector.tensor_tensor(
-                out=part, in0=part, in1=s_col[:].unsqueeze(1).to_broadcast([P, 256, 4]), op=MULT
-            )
+            for e in range(2):
+                pairs = banks["u", b][:, 2 * e : 2 * e + 2, :].bitcast(BF16)
+                lo = (2 * b + e) * 512
+                nc.vector.tensor_tensor(
+                    out=g_u[:, lo : lo + 512].rearrange("p (d u h) -> p d u h", u=2, h=2),
+                    in0=pairs.rearrange("p u (d h) -> p d u h", h=2),
+                    in1=s_col[:]
+                    .rearrange("p (u h) -> p u h", u=2)
+                    .unsqueeze(1)
+                    .to_broadcast([P, P, 2, 2]),
+                    op=MULT,
+                )
 
         def u_quantise(g):
             nc.vector.quantize_mx(
@@ -148,8 +150,8 @@ def tile_hybridsuperlayer_pa_t_kernel(tc, x, c_fc_U, c_fc_S, c_fc_V, c_fc_bias, 
         arranged = {}
 
         def arrange(n):
-            x_ar = xar.tile([P, len(ARRANGED), 512], U32, name="x_ar", tag="x_ar")
-            words = x_tiles[n][:].bitcast(U32).rearrange("p (j g w u) -> p j g w u", j=J, g=2, u=2)
+            x_ar = xar.tile([P, 2, 512], F32, name="x_ar", tag="x_ar")
+            words = x_tiles[n][:].bitcast(F32).rearrange("p (j g w u) -> p j g w u", j=J, g=2, u=2)
             for i, j in enumerate(ARRANGED):
                 nc.vector.tensor_copy(
                     out=x_ar[:, i, :].rearrange("p (g u w) -> p g w u", g=2, u=2), in_=words[:, j]
@@ -161,7 +163,7 @@ def tile_hybridsuperlayer_pa_t_kernel(tc, x, c_fc_U, c_fc_S, c_fc_V, c_fc_bias, 
             tp = ps_t.tile([P, 4, P], F32, name="tp_x", tag="t")
             for q in range(4):
                 if (n, j) in arranged:
-                    cols = arranged[n, j][:, q * P : (q + 1) * P].bitcast(F32)
+                    cols = arranged[n, j][:, q * P : (q + 1) * P]
                     nc.tensor.transpose(tp[:, q, :], cols, ident[:])
                     continue
                 lo = j * 512 + (q // 2) * 256 + q % 2
@@ -224,53 +226,48 @@ def tile_hybridsuperlayer_pa_t_kernel(tc, x, c_fc_U, c_fc_S, c_fc_V, c_fc_bias, 
             )
 
         u_flip(0)
-        u_copy(0, "S")
         u_flip(1)
-        u_copy(1, "V")
         u_scale(0)
         v_flip(0)
         v_copy(0, "S")
         v_flip(1)
         v_copy(1, "S")
         u_scale(1)
-        v_quantise()
         u_flip(2)
-        u_copy(2, "S")
-        u_quantise(0)
         u_flip(3)
-        u_copy(3, "S")
-        u_scale(2)
+        u_quantise(0)
+        v_quantise()
         flip(0, 0)
         regroup(0, 0, "S")
+        u_scale(2)
+        u_scale(3)
         for c in range(4):
             w_product(0, c)
-        u_scale(3)
+        u_quantise(1)
         w_copy(0, 0, "S")
         w_copy(0, 1, "V")
-        u_quantise(1)
         w_copy(0, 2, "S")
         w_copy(0, 3, "V")
         flip(0, 1)
         flip(0, 2)
-        flip(0, 3)
         for c in range(4):
             w_product(1, c)
         regroup(0, 1, "S")
         w_quantise(0)
-        quantise(0, 0, 2)
         w_copy(1, 0, "S")
         w_copy(1, 1, "V")
         w_copy(1, 2, "S")
         w_copy(1, 3, "V")
+        flip(0, 3)
         regroup(0, 2, "S")
+        quantise(0, 0, 2)
         w_quantise(1)
         regroup(0, 3, "S")
-        quantise(0, 2, 2)
         for j in range(J):
             flip(1, j)
-            regroup(1, j, "SV"[j % 2])
+            regroup(1, j, "S")
+        quantise(0, 2, 2)
         arrange(2)
-
 
         b_ps = ps_a.tile([P, DFF], F32, name="b_ps", tag="a")
         nc.tensor.matmul(out=b_ps[:], lhsT=ones[:], rhs=b_rows[:], start=True, stop=True)

@@ -56,7 +56,7 @@ def tile_hybridsuperlayer_pa_t_kernel(tc, x, c_fc_U, c_fc_S, c_fc_V, c_fc_bias, 
         b_rows = keep.tile([P, DFF], BF16, name="b_rows")
         ones = keep.tile([P, P], BF16, name="ones")
         warm = keep.tile([P, 8], F32, name="warm")
-        ident = keep.tile([P, P], F32, name="ident")
+        ident = keep.tile([P, P], F32, name="ident", align_bytes=256)
         nc.vector.memset(warm[:], 0.0)
         nc.vector.memset(b_rows[:], 0.0)
         nc.vector.memset(ones[:], 1.0)
@@ -76,7 +76,7 @@ def tile_hybridsuperlayer_pa_t_kernel(tc, x, c_fc_U, c_fc_S, c_fc_V, c_fc_bias, 
         x_tiles = {}
 
         def load(n, pieces=1):
-            x_sb = xin.tile([P, J * D], BF16, name="x_sb", tag="x_sb")
+            x_sb = xin.tile([P, J * D], BF16, name="x_sb", tag="x_sb", align_bytes=256)
             width = J * D // pieces
             for h in range(pieces):
                 cols = slice(h * width, (h + 1) * width)
@@ -150,7 +150,7 @@ def tile_hybridsuperlayer_pa_t_kernel(tc, x, c_fc_U, c_fc_S, c_fc_V, c_fc_bias, 
         arranged = {}
 
         def arrange(n):
-            x_ar = xar.tile([P, 2, 512], F32, name="x_ar", tag="x_ar")
+            x_ar = xar.tile([P, 2, 512], F32, name="x_ar", tag="x_ar", align_bytes=256)
             words = x_tiles[n][:].bitcast(F32).rearrange("p (j g w u) -> p j g w u", j=J, g=2, u=2)
             for i, j in enumerate(ARRANGED):
                 nc.vector.tensor_copy(
@@ -173,7 +173,7 @@ def tile_hybridsuperlayer_pa_t_kernel(tc, x, c_fc_U, c_fc_S, c_fc_V, c_fc_bias, 
 
         def regroup(n, j, engine):
             if j == 0:
-                g_x = xgr.tile([P, J * D], BF16, name="g_x", tag="g_x", align_bytes=64)
+                g_x = xgr.tile([P, J * D], BF16, name="g_x", tag="g_x", align_bytes=256)
                 grouped[n] = g_x
             g_x_words = (
                 grouped[n][:].bitcast(F32).rearrange("p (j g t u) -> p j g t u", j=J, g=2, t=P, u=2)
@@ -184,8 +184,8 @@ def tile_hybridsuperlayer_pa_t_kernel(tc, x, c_fc_U, c_fc_S, c_fc_V, c_fc_bias, 
 
         def quantise(n, first, count):
             if first == 0:
-                x_codes = xq.tile([P, J * 256], U32, name="x_codes", tag="x_codes", align_bytes=64)
-                x_scales = xq.tile([P, J * 256], U8, name="x_scales", tag="x_scales", align_bytes=64)
+                x_codes = xq.tile([P, J * 256], U32, name="x_codes", tag="x_codes", align_bytes=256)
+                x_scales = xq.tile([P, J * 256], U8, name="x_scales", tag="x_scales", align_bytes=256)
                 codes[n] = (x_codes, x_scales)
             x_codes, x_scales = codes[n]
             nc.vector.quantize_mx(
@@ -195,8 +195,8 @@ def tile_hybridsuperlayer_pa_t_kernel(tc, x, c_fc_U, c_fc_S, c_fc_V, c_fc_bias, 
             )
 
         g_w = keep.tile([P, 2, DFF, 4], BF16, name="g_w", align_bytes=64)
-        w_codes = keep.tile([P, 2, DFF], U32, name="w_codes", align_bytes=64)
-        w_scales = keep.tile([P, 2, DFF], U8, name="w_scales", align_bytes=64)
+        w_codes = keep.tile([P, 2, DFF], U32, name="w_codes", align_bytes=256)
+        w_scales = keep.tile([P, 2, DFF], U8, name="w_scales", align_bytes=256)
 
         def w_product(g, c):
             wa = ps_a.tile([P, 4, P], F32, name="wa", tag="a")

from contextlib import ExitStack

import concourse.mybir as mybir
from concourse.masks import make_identity

F32 = mybir.dt.float32
BF16 = mybir.dt.bfloat16
U32 = mybir.dt.uint32
U8 = mybir.dt.uint8
FP8X4 = mybir.dt.float8_e4m3fn_x4
GELU = mybir.ActivationFunctionType.Gelu
MULT = mybir.AluOpType.mult
ADD = mybir.AluOpType.add

P = 128
TOKENS = 8192
D = 1024
DFF = 512
RANK = 512
FLOPS = 2 * D * RANK * DFF + 2 * TOKENS * D * DFF

J = 4
NG = TOKENS // (P * J)
XBUFS = 8
LAG = 2
FINE_STORES = 1
ARRANGED = (1, 3)
LEAD = 2


def tile_hybridsuperlayer_pa_t_kernel(tc, x, c_fc_U, c_fc_S, c_fc_V, c_fc_bias, out):
    nc = tc.nc
    x_groups = x.flatten_outer_dims().rearrange("(n p j) k -> n p (j k)", p=P, j=J)
    out_groups = out.flatten_outer_dims().rearrange("(n p j) f -> n p (j f)", p=P, j=J)

    with ExitStack() as ctx:
        ctx.enter_context(tc.manual_schedule())
        keep = ctx.enter_context(tc.tile_pool(name="keep", bufs=1))
        xin = ctx.enter_context(tc.tile_pool(name="xin", bufs=XBUFS))
        xar = ctx.enter_context(tc.tile_pool(name="xar", bufs=2))
        xgr = ctx.enter_context(tc.tile_pool(name="xgr", bufs=3))
        xq = ctx.enter_context(tc.tile_pool(name="xq", bufs=4))
        res = ctx.enter_context(tc.tile_pool(name="res", bufs=6))
        ps_t = ctx.enter_context(tc.psum_pool(name="ps_t", bufs=4))
        ps_a = ctx.enter_context(tc.psum_pool(name="ps_a", bufs=4))

        def copy_on(engine, dst, src):
            if engine == "V":
                nc.vector.tensor_copy(out=dst, in_=src)
            else:
                nc.scalar.copy(out=dst, in_=src)

        u_sb = keep.tile([P, 4, 2 * RANK], BF16, name="u_sb")
        v_sb = keep.tile([P, 4, RANK], BF16, name="v_sb")
        s_col = keep.tile([P, 4], BF16, name="s_col")
        b_rows = keep.tile([P, DFF], BF16, name="b_rows")
        ones = keep.tile([P, P], BF16, name="ones")
        warm = keep.tile([P, 8], F32, name="warm")
        ident = keep.tile([P, P], F32, name="ident", align_bytes=256)
        nc.vector.memset(warm[:], 0.0)
        nc.vector.memset(b_rows[:], 0.0)
        nc.vector.memset(ones[:], 1.0)
        make_identity(nc, ident[:])

        u_view = c_fc_U.rearrange("(g p h e) r -> p g h (e r)", g=2, p=P, h=2, e=2)
        nc.scalar.dma_start(out=s_col[:], in_=c_fc_S.rearrange("(p t) -> p t", t=4))
        nc.scalar.activation(out=warm[:], in_=warm[:], func=GELU)
        nc.sync.dma_start(out=u_sb[:, 0:1, :], in_=u_view[:, 0, 0:1, :])
        nc.sync.dma_start(out=u_sb[:, 1:2, :], in_=u_view[:, 0, 1:2, :])
        v_view = c_fc_V.rearrange("(c p) r -> p c r", p=P)
        nc.sync.dma_start(out=v_sb[:, 0:2, :], in_=v_view[:, 0:2, :])
        nc.sync.dma_start(out=v_sb[:, 2:4, :], in_=v_view[:, 2:4, :])
        nc.sync.dma_start(out=b_rows[0:1, :], in_=c_fc_bias.rearrange("(o f) -> o f", o=1))
        nc.sync.dma_start(out=u_sb[:, 2:4, :], in_=u_view[:, 1, :, :])

        x_tiles = {}

        def load(n, pieces=1):
            x_sb = xin.tile([P, J * D], BF16, name="x_sb", tag="x_sb", align_bytes=256)
            width = J * D // pieces
            for h in range(pieces):
                cols = slice(h * width, (h + 1) * width)
                nc.sync.dma_start(out=x_sb[:, cols], in_=x_groups[n][:, cols])
            x_tiles[n] = x_sb

        for n in range(XBUFS):
            load(n, pieces=4 if n == 0 else 1)

        u_words = u_sb[:].bitcast(F32)
        v_words = v_sb[:].bitcast(F32)
        g_u = keep.tile([P, 8 * 512], BF16, name="g_u", align_bytes=64)
        g_v = keep.tile([P, 4 * 512], BF16, name="g_v", align_bytes=64)
        g_v_words = g_v[:].bitcast(F32).rearrange("p (c f u) -> p c f u", c=4, f=P, u=2)
        u_codes = keep.tile([P, 8 * P], U32, name="u_codes", align_bytes=64)
        u_scales = keep.tile([P, 8 * P], U8, name="u_scales", align_bytes=64)
        v_codes = keep.tile([P, DFF], U32, name="v_codes", align_bytes=64)
        v_scales = keep.tile([P, DFF], U8, name="v_scales", align_bytes=64)
        banks = {}

        def u_flip(b):
            tp = ps_t.tile([P, 4, P], F32, name="tp_u", tag="t")
            for e in range(2):
                for u in range(2):
                    nc.tensor.transpose(
                        tp[:, 2 * e + u, :], u_words[:, b, e * 256 + u : (e + 1) * 256 : 2], ident[:]
                    )
            banks["u", b] = tp

        def u_scale(b):
            for e in range(2):
                pairs = banks["u", b][:, 2 * e : 2 * e + 2, :].bitcast(BF16)
                lo = (2 * b + e) * 512
                nc.vector.tensor_tensor(
                    out=g_u[:, lo : lo + 512].rearrange("p (d u h) -> p d u h", u=2, h=2),
                    in0=pairs.rearrange("p u (d h) -> p d u h", h=2),
                    in1=s_col[:]
                    .rearrange("p (u h) -> p u h", u=2)
                    .unsqueeze(1)
                    .to_broadcast([P, P, 2, 2]),
                    op=MULT,
                )

        def u_quantise(g):
            nc.vector.quantize_mx(
                out=u_codes[:, 512 * g : 512 * (g + 1)].bitcast(FP8X4),
                scales=u_scales[:, 512 * g : 512 * (g + 1)],
                in_=g_u[:, 2048 * g : 2048 * (g + 1)],
            )

        def v_flip(b):
            tp = ps_t.tile([P, 4, P], F32, name="tp_v", tag="t")
            for cc in range(2):
                for u in range(2):
                    nc.tensor.transpose(tp[:, 2 * cc + u, :], v_words[:, 2 * b + cc, u::2], ident[:])
            banks["v", b] = tp

        def v_copy(b, engine):
            copy_on(
                engine,
                g_v_words[:, 2 * b : 2 * b + 2],
                banks["v", b][:].rearrange("p (c u) f -> p c f u", u=2),
            )

        def v_quantise():
            nc.vector.quantize_mx(out=v_codes[:].bitcast(FP8X4), scales=v_scales[:], in_=g_v[:])

        grouped = {}
        codes = {}

        arranged = {}

        def arrange(n):
            x_ar = xar.tile([P, 2, 512], F32, name="x_ar", tag="x_ar", align_bytes=256)
            words = x_tiles[n][:].bitcast(F32).rearrange("p (j g w u) -> p j g w u", j=J, g=2, u=2)
            for i, j in enumerate(ARRANGED):
                nc.vector.tensor_copy(
                    out=x_ar[:, i, :].rearrange("p (g u w) -> p g w u", g=2, u=2), in_=words[:, j]
                )
                arranged[n, j] = x_ar[:, i, :]

        def flip(n, j):
            words = x_tiles[n][:].bitcast(F32)
            tp = ps_t.tile([P, 4, P], F32, name="tp_x", tag="t")
            for q in range(4):
                if (n, j) in arranged:
                    cols = arranged[n, j][:, q * P : (q + 1) * P]
                    nc.tensor.transpose(tp[:, q, :], cols, ident[:])
                    continue
                lo = j * 512 + (q // 2) * 256 + q % 2
                hi = j * 512 + (q // 2 + 1) * 256
                nc.tensor.transpose(tp[:, q, :], words[:, lo:hi:2], ident[:])
            banks["x", n, j] = tp

        def regroup(n, j, engine):
            if j == 0:
                g_x = xgr.tile([P, J * D], BF16, name="g_x", tag="g_x", align_bytes=256)
                grouped[n] = g_x
            g_x_words = (
                grouped[n][:].bitcast(F32).rearrange("p (j g t u) -> p j g t u", j=J, g=2, t=P, u=2)
            )
            copy_on(engine, g_x_words[:, j], banks["x", n, j][:].rearrange("p (g u) t -> p g t u", u=2))
            if j == J - 1 and n + XBUFS < NG:
                load(n + XBUFS)

        def quantise(n, first, count):
            if first == 0:
                x_codes = xq.tile([P, J * 256], U32, name="x_codes", tag="x_codes", align_bytes=256)
                x_scales = xq.tile([P, J * 256], U8, name="x_scales", tag="x_scales", align_bytes=256)
                codes[n] = (x_codes, x_scales)
            x_codes, x_scales = codes[n]
            nc.vector.quantize_mx(
                out=x_codes[:, first * 256 : (first + count) * 256].bitcast(FP8X4),
                scales=x_scales[:, first * 256 : (first + count) * 256],
                in_=grouped[n][:, first * D : (first + count) * D],
            )

        g_w = keep.tile([P, 2, DFF, 4], BF16, name="g_w", align_bytes=64)
        w_codes = keep.tile([P, 2, DFF], U32, name="w_codes", align_bytes=256)
        w_scales = keep.tile([P, 2, DFF], U8, name="w_scales", align_bytes=256)

        def w_product(g, c):
            wa = ps_a.tile([P, 4, P], F32, name="wa", tag="a")
            for t in range(4):
                lo = (4 * g + t) * P
                nc.tensor.matmul_mx(
                    out=wa[:, t, :],
                    lhsT=u_codes[:, lo : lo + P].bitcast(FP8X4),
                    lhsT_scale=u_scales[:, lo : lo + P],
                    rhs=v_codes[:, c * P : (c + 1) * P].bitcast(FP8X4),
                    rhs_scale=v_scales[:, c * P : (c + 1) * P],
                    start=True,
                    stop=True,
                )
            banks["w", g, c] = wa

        def w_copy(g, c, engine):
            copy_on(
                engine, g_w[:, g, c * P : (c + 1) * P, :], banks["w", g, c][:].rearrange("p t f -> p f t")
            )

        def w_quantise(g):
            nc.vector.quantize_mx(
                out=w_codes[:, g, :].bitcast(FP8X4),
                scales=w_scales[:, g, :],
                in_=g_w[:, g].rearrange("p f t -> p (f t)"),
            )

        u_flip(0)
        u_flip(1)
        u_scale(0)
        v_flip(0)
        v_copy(0, "S")
        v_flip(1)
        v_copy(1, "S")
        u_scale(1)
        u_flip(2)
        u_flip(3)
        u_quantise(0)
        v_quantise()
        flip(0, 0)
        regroup(0, 0, "S")
        u_scale(2)
        u_scale(3)
        for c in range(4):
            w_product(0, c)
        u_quantise(1)
        w_copy(0, 0, "S")
        w_copy(0, 1, "V")
        w_copy(0, 2, "S")
        w_copy(0, 3, "V")
        flip(0, 1)
        flip(0, 2)
        for c in range(4):
            w_product(1, c)
        regroup(0, 1, "S")
        w_quantise(0)
        w_copy(1, 0, "S")
        w_copy(1, 1, "V")
        w_copy(1, 2, "S")
        w_copy(1, 3, "V")
        flip(0, 3)
        regroup(0, 2, "S")
        quantise(0, 0, 2)
        w_quantise(1)
        regroup(0, 3, "S")
        for j in range(J):
            flip(1, j)
            regroup(1, j, "S")
        quantise(0, 2, 2)
        arrange(2)

        b_ps = ps_a.tile([P, DFF], F32, name="b_ps", tag="a")
        nc.tensor.matmul(out=b_ps[:], lhsT=ones[:], rhs=b_rows[:], start=True, stop=True)
        bias_bc = keep.tile([P, DFF], F32, name="bias_bc")
        nc.scalar.copy(out=bias_bc[:], in_=b_ps[:])

        waiting = []

        def product(n, o_sb, j):
            x_codes, x_scales = codes[n]
            acc = ps_a.tile([P, DFF], F32, name="acc", tag="a")
            for g in range(2):
                lo = (2 * j + g) * P
                nc.tensor.matmul_mx(
                    out=acc[:],
                    lhsT=x_codes[:, lo : lo + P].bitcast(FP8X4),
                    lhsT_scale=x_scales[:, lo : lo + P],
                    rhs=w_codes[:, g, :].bitcast(FP8X4),
                    rhs_scale=w_scales[:, g, :],
                    start=(g == 0),
                    stop=(g == 1),
                )
            pieces = 2 if (n == NG - 1 and j == J - 1) else 1
            width = DFF // pieces
            for h in range(pieces):
                nc.vector.tensor_tensor(
                    out=o_sb[:, j * DFF + h * width : j * DFF + (h + 1) * width],
                    in0=acc[:, h * width : (h + 1) * width],
                    in1=bias_bc[:, h * width : (h + 1) * width],
                    op=ADD,
                )
            waiting.append((n, o_sb, j, pieces))

        def finish(i):
            n, o_sb, j, pieces = waiting[i]
            width = DFF // pieces
            for h in range(pieces):
                lo = j * DFF + h * width
                cols = o_sb[:, lo : lo + width]
                nc.scalar.activation(out=cols, in_=cols, func=GELU)
                if n >= NG - FINE_STORES:
                    nc.sync.dma_start(out=out_groups[n][:, lo : lo + width], in_=cols)
            if n < NG - FINE_STORES and j % 2 == 1:
                both = slice((j - 1) * DFF, (j + 1) * DFF)
                nc.sync.dma_start(out=out_groups[n][:, both], in_=o_sb[:, both])

        def multiply_group(n):
            o_sb = res.tile([P, J * DFF], F32, name="o_sb", tag="o_sb")
            for j in range(J):
                product(n, o_sb, j)
                if n * J + j >= LAG:
                    finish(n * J + j - LAG)

        def transpose_group(n, engines):
            for j in range(J):
                flip(n, j)
                regroup(n, j, engines[j])

        multiply_group(0)
        quantise(1, 0, J)
        transpose_group(2, "SSSS")
        arrange(3)
        for n in range(1, NG):
            if n + 1 < NG:
                quantise(n + 1, 0, J)
            if n + LEAD < NG:
                transpose_group(n + LEAD, "SSSV" if n % 3 == 1 else "SSSS")
            if n + LEAD + 1 < NG:
                arrange(n + LEAD + 1)
            multiply_group(n)
        for i in range(NG * J - LAG, NG * J):
            finish(i)
